import numpy as np
import ml_dtypes


def mxq(x, axis, fmt="e4m3"):
    dtype, down = {"e4m3": (ml_dtypes.float8_e4m3fn, 7), "e5m2": (ml_dtypes.float8_e5m2, 14)}[fmt]
    v = np.moveaxis(np.asarray(x, np.float32).astype(ml_dtypes.bfloat16).astype(np.float64), axis, -1)
    blocks = v.reshape(v.shape[:-1] + (-1, 32))
    amax = np.abs(blocks).max(-1, keepdims=True)
    byte = np.maximum(np.where(amax > 0, np.frexp(amax)[1] - 1 + 127, 0) - down, 1)
    scale = np.exp2(byte - 127.0)
    codes = (blocks / scale).astype(np.float32).astype(dtype).astype(np.float64)
    return np.moveaxis((codes * scale).reshape(v.shape), -1, axis)


WIDE = False


def mx_kscale(k, group=512):
    if not WIDE:
        return np.ones(k)
    levels = np.array([10, -10, 5, -5, 0])
    if group != 512:
        return np.exp2(np.random.permutation(np.resize(levels, k // group))).repeat(group)
    a = np.random.permutation(np.resize(levels, k // 512 * 4)).reshape(k // 512, 4)
    idx = np.arange(k)
    return np.exp2(a[idx // 512, idx % 128 // 32])


BF16 = ml_dtypes.bfloat16


def bf(x):
    return np.asarray(x, np.float32).astype(BF16)


def f64(x):
    return np.asarray(x).astype(np.float64)


B, T, D, F = 8, 512, 4096, 128
TRIPLES = [(1, 2, 3), (1, 4, 5), (1, 7, 6), (2, 4, 6), (2, 5, 7), (3, 4, 7), (3, 6, 5)]
O = len(TRIPLES) + 1
D8, F8 = D // O, F // O


def oct_table():
    tab = [[None] * O for _ in range(O)]
    tab[0][0] = (0, 1.0)
    for i in range(1, O):
        tab[i][i] = (0, 1.0)
        tab[0][i] = (i, 1.0)
        tab[i][0] = (i, -1.0)
    for a, b, c in TRIPLES:
        for p, q, r in ((a, b, c), (b, c, a), (c, a, b)):
            tab[q][r] = (p, 1.0)
            tab[p][r] = (q, -1.0)
    return tab


def oct_linear(xq, w):
    tab = oct_table()
    p = (xq @ mxq(w.reshape(F, D8).T, 0, "e4m3")).reshape(B, T, O, O, F8)
    return np.concatenate([sum(tab[i][k][1] * p[:, :, i, tab[i][k][0]] for i in range(O)) for k in range(O)], axis=2)


def silu(v):
    return v / (1.0 + np.exp(-v))


def setup_inputs():
    s8 = mx_kscale(D8, D8 // 2)
    return {"x": bf(np.random.standard_normal((B, T, D)) * np.tile(s8, O)),
            "wq_gate": bf(np.random.standard_normal((O, F8, D8)) / np.sqrt(D) / s8),
            "wq_up": bf(np.random.standard_normal((O, F8, D8)) / np.sqrt(D) / s8)}


def reference(x, wq_gate, wq_up):
    xq = mxq(f64(x).reshape(B, T, O, D8), 3, "e4m3")
    gate = oct_linear(xq, f64(wq_gate))
    up = oct_linear(xq, f64(wq_up))
    return silu(gate) * up

@@ -1,0 +1,181 @@
+from contextlib import ExitStack
+
+import concourse.mybir as mybir
+from concourse.masks import make_identity
+
+F32 = mybir.dt.float32
+BF16 = mybir.dt.bfloat16
+U32 = mybir.dt.uint32
+U8 = mybir.dt.uint8
+FP8X4 = mybir.dt.float8_e4m3fn_x4
+SILU = mybir.ActivationFunctionType.Silu
+MULT = mybir.AluOpType.mult
+
+P = 128
+PACK = 4
+UNITS = 8
+COMP = 512
+O16 = 16
+F_OUT = UNITS * O16
+SIDES = 2
+GROUP = 4
+TRIPLES = [(1, 2, 3), (1, 4, 5), (1, 7, 6), (2, 4, 6), (2, 5, 7), (3, 4, 7), (3, 6, 5)]
+
+FLOPS = 2 * 4096 * 4096 * SIDES * F_OUT
+
+PREFETCH = 5
+LAG_QUANTISE = 1
+LAG_MATMUL = 2
+BANK_COMPS = 2
+BANKS = UNITS // BANK_COMPS
+
+
+def octonion_table():
+    table = {(0, 0): (0, 1.0)}
+    for i in range(1, UNITS):
+        table[(i, i)] = (0, 1.0)
+        table[(0, i)] = (i, 1.0)
+        table[(i, 0)] = (i, -1.0)
+    for a, b, c in TRIPLES:
+        for p, q, r in ((a, b, c), (b, c, a), (c, a, b)):
+            table[(q, r)] = (p, 1.0)
+            table[(p, r)] = (q, -1.0)
+    return table
+
+
+def tile_swiglumlp_pa_t_kernel(tc, x, wq_gate, wq_up, out):
+    nc = tc.nc
+    groups = x.shape[0]
+    n_tiles = groups * GROUP
+    features = UNITS * COMP
+    x_view = x.rearrange("g (p t) k -> g t p k", t=GROUP)
+    out_view = out.rearrange("g (p t) f -> g p (t f)", t=GROUP)
+    table = octonion_table()
+
+    with ExitStack() as ctx:
+        const = ctx.enter_context(tc.tile_pool(name="const", bufs=1))
+        x_pool = ctx.enter_context(tc.tile_pool(name="x_pool", bufs=PREFETCH + 1))
+        grouped_pool = ctx.enter_context(tc.tile_pool(name="grouped_pool", bufs=3))
+        codes_pool = ctx.enter_context(tc.tile_pool(name="codes_pool", bufs=3))
+        result_pool = ctx.enter_context(tc.tile_pool(name="result_pool", bufs=3))
+        psum_t = ctx.enter_context(tc.psum_pool(name="psum_t", bufs=6))
+        psum_acc = ctx.enter_context(tc.psum_pool(name="psum_acc", bufs=2))
+        ctx.enter_context(tc.manual_schedule())
+
+        def load(r):
+            x_sb = x_pool.tile([P, features], BF16, name="x_sb")
+            nc.sync.dma_start(out=x_sb[:], in_=x_view[r // GROUP, r % GROUP])
+            return x_sb
+
+        w_raw = const.tile([P, SIDES * COMP], BF16, name="w_raw")
+        nc.sync.dma_start(out=w_raw[:, 0:COMP], in_=wq_gate.rearrange("j o d -> (j o) d"))
+        nc.sync.dma_start(out=w_raw[:, COMP : 2 * COMP], in_=wq_up.rearrange("j o d -> (j o) d"))
+        x_tiles = {}
+        for r in range(PREFETCH):
+            x_tiles[r] = load(r)
+
+        ident = const.tile([P, P], F32, name="ident")
+        make_identity(nc, ident[:])
+        warm = const.tile([P, 1], F32, name="warm")
+        nc.vector.memset(warm[:], 0.0)
+        nc.scalar.activation(out=warm[:], in_=warm[:], func=SILU)
+
+        w_words = w_raw[:].bitcast(F32).rearrange("p (s w u) -> p s u w", s=SIDES, u=2)
+        wt = psum_t.tile([P, SIDES, 2, P], F32, name="xt")
+        for s in range(SIDES):
+            for u in range(2):
+                nc.tensor.transpose(wt[:, s, u, :], w_words[:, s, u, :], ident[:])
+        w_grouped = const.tile([P, UNITS * SIDES * F_OUT * PACK], BF16, name="w_grouped", align_bytes=64)
+        w_grouped_words = w_grouped[:].bitcast(F32).rearrange(
+            "p (i s c u) -> p i s c u", i=UNITS, s=SIDES, u=2
+        )
+        nc.vector.tensor_copy(out=w_grouped_words[:, 0], in_=wt[:].rearrange("p s u c -> p s c u"))
+        w_blocks = w_grouped[:].rearrange("p (i s k e) -> p i s k e", i=UNITS, s=SIDES, k=UNITS)
+        for i in range(1, UNITS):
+            for k in range(UNITS):
+                j, sign = table[(i, k)]
+                if i % 3 == 1:
+                    nc.scalar.mul(w_blocks[:, i, :, k, :], w_blocks[:, 0, :, j, :], sign)
+                else:
+                    nc.vector.tensor_scalar_mul(
+                        out=w_blocks[:, i, :, k, :], in0=w_blocks[:, 0, :, j, :], scalar1=sign
+                    )
+        n_cols = SIDES * F_OUT
+        w_codes = const.tile([P, UNITS * n_cols], U32, name="w_codes", align_bytes=64)
+        w_scales = const.tile([P, UNITS * n_cols], U8, name="w_scales", align_bytes=64)
+        half = UNITS * n_cols // 2
+        for h in range(2):
+            nc.vector.quantize_mx(
+                out=w_codes[:, h * half : (h + 1) * half].bitcast(FP8X4),
+                scales=w_scales[:, h * half : (h + 1) * half],
+                in_=w_grouped[:, h * half * PACK : (h + 1) * half * PACK],
+            )
+
+        grouped_tiles = {}
+        code_tiles = {}
+        out_tiles = {}
+
+        def transpose_and_regroup(r):
+            words = x_tiles[r][:].bitcast(F32).rearrange("p (c w u) -> p c u w", c=UNITS, u=2)
+            grouped = grouped_pool.tile([P, features], BF16, name="grouped", align_bytes=64)
+            grouped_words = grouped[:].bitcast(F32).rearrange("p (c r u) -> p c r u", c=UNITS, u=2)
+            banks = []
+            for b in range(BANKS):
+                xt = psum_t.tile([P, BANK_COMPS, 2, P], F32, name="xt")
+                for c in range(BANK_COMPS):
+                    for u in range(2):
+                        nc.tensor.transpose(xt[:, c, u, :], words[:, b * BANK_COMPS + c, u, :], ident[:])
+                banks.append(xt)
+            for b in range(BANKS):
+                dst = grouped_words[:, b * BANK_COMPS : (b + 1) * BANK_COMPS]
+                src = banks[b][:].rearrange("p c u r -> p c r u")
+                if b == BANKS - 1:
+                    nc.vector.tensor_copy(out=dst, in_=src)
+                else:
+                    nc.scalar.copy(out=dst, in_=src)
+            grouped_tiles[r] = grouped
+
+        def quantise(r):
+            codes = codes_pool.tile([P, UNITS * P], U32, name="codes", align_bytes=64)
+            scales = codes_pool.tile([P, UNITS * P], U8, name="scales", align_bytes=64)
+            nc.vector.quantize_mx(
+                out=codes[:].bitcast(FP8X4), scales=scales[:], in_=grouped_tiles[r][:]
+            )
+            code_tiles[r] = (codes, scales)
+
+        def multiply_and_gate(r):
+            codes, scales = code_tiles[r]
+            acc = psum_acc.tile([P, n_cols], F32, name="acc")
+            for i in range(UNITS):
+                nc.tensor.matmul_mx(
+                    out=acc[:],
+                    lhsT=codes[:, i * P : (i + 1) * P].bitcast(FP8X4),
+                    lhsT_scale=scales[:, i * P : (i + 1) * P],
+                    rhs=w_codes[:, i * n_cols : (i + 1) * n_cols].bitcast(FP8X4),
+                    rhs_scale=w_scales[:, i * n_cols : (i + 1) * n_cols],
+                    start=(i == 0),
+                    stop=(i == UNITS - 1),
+                )
+            g, t = r // GROUP, r % GROUP
+            if t == 0:
+                out_tiles[g] = result_pool.tile([P, GROUP * F_OUT], F32, name="out_sb")
+            gate = result_pool.tile([P, F_OUT], F32, name="gate")
+            nc.scalar.activation(out=gate[:], in_=acc[:, 0:F_OUT], func=SILU)
+            nc.vector.tensor_tensor(
+                out=out_tiles[g][:, t * F_OUT : (t + 1) * F_OUT],
+                in0=gate[:],
+                in1=acc[:, F_OUT : 2 * F_OUT],
+                op=MULT,
+            )
+            if t == GROUP - 1:
+                nc.sync.dma_start(out=out_view[g], in_=out_tiles[g][:])
+
+        for step in range(n_tiles + LAG_MATMUL):
+            if step + PREFETCH < n_tiles:
+                x_tiles[step + PREFETCH] = load(step + PREFETCH)
+            if 0 <= step - LAG_QUANTISE < n_tiles:
+                quantise(step - LAG_QUANTISE)
+            if step < n_tiles:
+                transpose_and_regroup(step)
+            if step >= LAG_MATMUL:
+                multiply_and_gate(step - LAG_MATMUL)

@@ -55,6 +55,7 @@ def tile_swiglumlp_pa_t_kernel(tc, x, wq_gate, wq_up, out):
     with ExitStack() as ctx:
         const = ctx.enter_context(tc.tile_pool(name="const", bufs=1))
         x_pool = ctx.enter_context(tc.tile_pool(name="x_pool", bufs=PREFETCH + 1))
+        sorted_pool = ctx.enter_context(tc.tile_pool(name="sorted_pool", bufs=3))
         grouped_pool = ctx.enter_context(tc.tile_pool(name="grouped_pool", bufs=3))
         codes_pool = ctx.enter_context(tc.tile_pool(name="codes_pool", bufs=3))
         result_pool = ctx.enter_context(tc.tile_pool(name="result_pool", bufs=3))
@@ -104,19 +105,29 @@ def tile_swiglumlp_pa_t_kernel(tc, x, wq_gate, wq_up, out):
         w_codes = const.tile([P, UNITS * n_cols], U32, name="w_codes", align_bytes=64)
         w_scales = const.tile([P, UNITS * n_cols], U8, name="w_scales", align_bytes=64)
         half = UNITS * n_cols // 2
-        for h in range(2):
+
+        def quantise_weights(h):
             nc.vector.quantize_mx(
                 out=w_codes[:, h * half : (h + 1) * half].bitcast(FP8X4),
                 scales=w_scales[:, h * half : (h + 1) * half],
                 in_=w_grouped[:, h * half * PACK : (h + 1) * half * PACK],
             )
 
+        sorted_tiles = {}
         grouped_tiles = {}
         code_tiles = {}
         out_tiles = {}
 
+        def sort_words(r):
+            sorted_words = sorted_pool.tile([P, UNITS, 2, P], F32, name="sorted_words")
+            nc.vector.tensor_copy(
+                out=sorted_words[:],
+                in_=x_tiles[r][:].bitcast(F32).rearrange("p (c w u) -> p c u w", c=UNITS, u=2),
+            )
+            sorted_tiles[r] = sorted_words
+
         def transpose_and_regroup(r):
-            words = x_tiles[r][:].bitcast(F32).rearrange("p (c w u) -> p c u w", c=UNITS, u=2)
+            words = sorted_tiles[r]
             grouped = grouped_pool.tile([P, features], BF16, name="grouped", align_bytes=64)
             grouped_words = grouped[:].bitcast(F32).rearrange("p (c r u) -> p c r u", c=UNITS, u=2)
             banks = []
@@ -129,10 +140,7 @@ def tile_swiglumlp_pa_t_kernel(tc, x, wq_gate, wq_up, out):
             for b in range(BANKS):
                 dst = grouped_words[:, b * BANK_COMPS : (b + 1) * BANK_COMPS]
                 src = banks[b][:].rearrange("p c u r -> p c r u")
-                if b == BANKS - 1:
-                    nc.vector.tensor_copy(out=dst, in_=src)
-                else:
-                    nc.scalar.copy(out=dst, in_=src)
+                nc.scalar.copy(out=dst, in_=src)
             grouped_tiles[r] = grouped
 
         def quantise(r):
@@ -170,9 +178,14 @@ def tile_swiglumlp_pa_t_kernel(tc, x, wq_gate, wq_up, out):
             if t == GROUP - 1:
                 nc.sync.dma_start(out=out_view[g], in_=out_tiles[g][:])
 
+        sort_words(0)
         for step in range(n_tiles + LAG_MATMUL):
             if step + PREFETCH < n_tiles:
                 x_tiles[step + PREFETCH] = load(step + PREFETCH)
+            if step + 1 < n_tiles:
+                sort_words(step + 1)
+            if step < 2:
+                quantise_weights(step)
             if 0 <= step - LAG_QUANTISE < n_tiles:
                 quantise(step - LAG_QUANTISE)
             if step < n_tiles:

@@ -28,6 +28,8 @@ LAG_QUANTISE = 1
 LAG_MATMUL = 2
 BANK_COMPS = 2
 BANKS = UNITS // BANK_COMPS
+QUARTERS = 4
+QUARTER = 64
 
 
 def octonion_table():
@@ -81,11 +83,16 @@ def tile_swiglumlp_pa_t_kernel(tc, x, wq_gate, wq_up, out):
         nc.vector.memset(warm[:], 0.0)
         nc.scalar.activation(out=warm[:], in_=warm[:], func=SILU)
 
-        w_words = w_raw[:].bitcast(F32).rearrange("p (s w u) -> p s u w", s=SIDES, u=2)
+        w_words = w_raw[:].bitcast(F32).rearrange("p (s q w) -> p s q w", s=SIDES, q=QUARTERS)
+        w_outer = const.tile([P, SIDES, 2, QUARTER], F32, name="w_outer")
+        nc.vector.tensor_copy(out=w_outer[:], in_=w_words[:, :, 0 : QUARTERS : QUARTERS - 1, :])
+        w_flat = w_raw[:].bitcast(F32)
         wt = psum_t.tile([P, SIDES, 2, P], F32, name="xt")
         for s in range(SIDES):
-            for u in range(2):
-                nc.tensor.transpose(wt[:, s, u, :], w_words[:, s, u, :], ident[:])
+            nc.tensor.transpose(wt[:, s, 0, :], w_outer[:, s].rearrange("p h w -> p (h w)"), ident[:])
+            nc.tensor.transpose(
+                wt[:, s, 1, :], w_flat[:, s * 2 * P + QUARTER : s * 2 * P + 3 * QUARTER], ident[:]
+            )
         w_grouped = const.tile([P, UNITS * SIDES * F_OUT * PACK], BF16, name="w_grouped", align_bytes=64)
         w_grouped_words = w_grouped[:].bitcast(F32).rearrange(
             "p (i s c u) -> p i s c u", i=UNITS, s=SIDES, u=2
@@ -119,23 +126,29 @@ def tile_swiglumlp_pa_t_kernel(tc, x, wq_gate, wq_up, out):
         out_tiles = {}
 
         def sort_words(r):
-            sorted_words = sorted_pool.tile([P, UNITS, 2, P], F32, name="sorted_words")
+            sorted_words = sorted_pool.tile([P, UNITS, 2, QUARTER], F32, name="sorted_words")
             nc.vector.tensor_copy(
                 out=sorted_words[:],
-                in_=x_tiles[r][:].bitcast(F32).rearrange("p (c w u) -> p c u w", c=UNITS, u=2),
+                in_=x_tiles[r][:].bitcast(F32).rearrange("p (c q w) -> p c q w", c=UNITS, q=QUARTERS)[
+                    :, :, 0 : QUARTERS : QUARTERS - 1, :
+                ],
             )
             sorted_tiles[r] = sorted_words
 
         def transpose_and_regroup(r):
-            words = sorted_tiles[r]
+            outer = sorted_tiles[r]
+            inner = x_tiles[r][:].bitcast(F32)
             grouped = grouped_pool.tile([P, features], BF16, name="grouped", align_bytes=64)
             grouped_words = grouped[:].bitcast(F32).rearrange("p (c r u) -> p c r u", c=UNITS, u=2)
             banks = []
             for b in range(BANKS):
                 xt = psum_t.tile([P, BANK_COMPS, 2, P], F32, name="xt")
                 for c in range(BANK_COMPS):
-                    for u in range(2):
-                        nc.tensor.transpose(xt[:, c, u, :], words[:, b * BANK_COMPS + c, u, :], ident[:])
+                    comp = b * BANK_COMPS + c
+                    nc.tensor.transpose(xt[:, c, 0, :], outer[:, comp].rearrange("p h w -> p (h w)"), ident[:])
+                    nc.tensor.transpose(
+                        xt[:, c, 1, :], inner[:, comp * 2 * P + QUARTER : comp * 2 * P + 3 * QUARTER], ident[:]
+                    )
                 banks.append(xt)
             for b in range(BANKS):
                 dst = grouped_words[:, b * BANK_COMPS : (b + 1) * BANK_COMPS]

@@ -23,9 +23,9 @@ TRIPLES = [(1, 2, 3), (1, 4, 5), (1, 7, 6), (2, 4, 6), (2, 5, 7), (3, 4, 7), (3,
 
 FLOPS = 2 * 4096 * 4096 * SIDES * F_OUT
 
-PREFETCH = 5
-LAG_QUANTISE = 1
-LAG_MATMUL = 2
+X_BUFS = 8
+PAIR = 2
+T_BANKS = 7
 BANK_COMPS = 2
 BANKS = UNITS // BANK_COMPS
 QUARTERS = 4
@@ -56,13 +56,13 @@ def tile_swiglumlp_pa_t_kernel(tc, x, wq_gate, wq_up, out):
 
     with ExitStack() as ctx:
         const = ctx.enter_context(tc.tile_pool(name="const", bufs=1))
-        x_pool = ctx.enter_context(tc.tile_pool(name="x_pool", bufs=PREFETCH + 1))
-        sorted_pool = ctx.enter_context(tc.tile_pool(name="sorted_pool", bufs=3))
-        grouped_pool = ctx.enter_context(tc.tile_pool(name="grouped_pool", bufs=3))
-        codes_pool = ctx.enter_context(tc.tile_pool(name="codes_pool", bufs=3))
+        x_pool = ctx.enter_context(tc.tile_pool(name="x_pool", bufs=X_BUFS))
+        sorted_pool = ctx.enter_context(tc.tile_pool(name="sorted_pool", bufs=4))
+        grouped_pool = ctx.enter_context(tc.tile_pool(name="grouped_pool", bufs=4))
+        codes_pool = ctx.enter_context(tc.tile_pool(name="codes_pool", bufs=4))
         result_pool = ctx.enter_context(tc.tile_pool(name="result_pool", bufs=3))
-        psum_t = ctx.enter_context(tc.psum_pool(name="psum_t", bufs=6))
-        psum_acc = ctx.enter_context(tc.psum_pool(name="psum_acc", bufs=2))
+        psum_t = ctx.enter_context(tc.psum_pool(name="psum_t", bufs=T_BANKS))
+        psum_acc = ctx.enter_context(tc.psum_pool(name="psum_acc", bufs=1))
         ctx.enter_context(tc.manual_schedule())
 
         def load(r):
@@ -74,7 +74,7 @@ def tile_swiglumlp_pa_t_kernel(tc, x, wq_gate, wq_up, out):
         nc.sync.dma_start(out=w_raw[:, 0:COMP], in_=wq_gate.rearrange("j o d -> (j o) d"))
         nc.sync.dma_start(out=w_raw[:, COMP : 2 * COMP], in_=wq_up.rearrange("j o d -> (j o) d"))
         x_tiles = {}
-        for r in range(PREFETCH):
+        for r in range(X_BUFS):
             x_tiles[r] = load(r)
 
         ident = const.tile([P, P], F32, name="ident")
@@ -123,6 +123,8 @@ def tile_swiglumlp_pa_t_kernel(tc, x, wq_gate, wq_up, out):
         sorted_tiles = {}
         grouped_tiles = {}
         code_tiles = {}
+        acc_tiles = {}
+        gate_tiles = {}
         out_tiles = {}
 
         def sort_words(r):
@@ -135,7 +137,7 @@ def tile_swiglumlp_pa_t_kernel(tc, x, wq_gate, wq_up, out):
             )
             sorted_tiles[r] = sorted_words
 
-        def transpose_and_regroup(r):
+        def transpose_and_regroup(r, vector_banks):
             outer = sorted_tiles[r]
             inner = x_tiles[r][:].bitcast(F32)
             grouped = grouped_pool.tile([P, features], BF16, name="grouped", align_bytes=64)
@@ -153,7 +155,10 @@ def tile_swiglumlp_pa_t_kernel(tc, x, wq_gate, wq_up, out):
             for b in range(BANKS):
                 dst = grouped_words[:, b * BANK_COMPS : (b + 1) * BANK_COMPS]
                 src = banks[b][:].rearrange("p c u r -> p c r u")
-                nc.scalar.copy(out=dst, in_=src)
+                if b in vector_banks:
+                    nc.vector.tensor_copy(out=dst, in_=src)
+                else:
+                    nc.scalar.copy(out=dst, in_=src)
             grouped_tiles[r] = grouped
 
         def quantise(r):
@@ -164,44 +169,66 @@ def tile_swiglumlp_pa_t_kernel(tc, x, wq_gate, wq_up, out):
             )
             code_tiles[r] = (codes, scales)
 
-        def multiply_and_gate(r):
-            codes, scales = code_tiles[r]
-            acc = psum_acc.tile([P, n_cols], F32, name="acc")
-            for i in range(UNITS):
-                nc.tensor.matmul_mx(
-                    out=acc[:],
-                    lhsT=codes[:, i * P : (i + 1) * P].bitcast(FP8X4),
-                    lhsT_scale=scales[:, i * P : (i + 1) * P],
-                    rhs=w_codes[:, i * n_cols : (i + 1) * n_cols].bitcast(FP8X4),
-                    rhs_scale=w_scales[:, i * n_cols : (i + 1) * n_cols],
-                    start=(i == 0),
-                    stop=(i == UNITS - 1),
-                )
-            g, t = r // GROUP, r % GROUP
-            if t == 0:
-                out_tiles[g] = result_pool.tile([P, GROUP * F_OUT], F32, name="out_sb")
-            gate = result_pool.tile([P, F_OUT], F32, name="gate")
-            nc.scalar.activation(out=gate[:], in_=acc[:, 0:F_OUT], func=SILU)
+        def multiply(j):
+            acc = psum_acc.tile([P, PAIR, n_cols], F32, name="acc")
+            for h in range(PAIR):
+                codes, scales = code_tiles[j * PAIR + h]
+                for i in range(UNITS):
+                    nc.tensor.matmul_mx(
+                        out=acc[:, h, :],
+                        lhsT=codes[:, i * P : (i + 1) * P].bitcast(FP8X4),
+                        lhsT_scale=scales[:, i * P : (i + 1) * P],
+                        rhs=w_codes[:, i * n_cols : (i + 1) * n_cols].bitcast(FP8X4),
+                        rhs_scale=w_scales[:, i * n_cols : (i + 1) * n_cols],
+                        start=(i == 0),
+                        stop=(i == UNITS - 1),
+                    )
+            acc_tiles[j] = acc
+
+        def silu(j):
+            gate = result_pool.tile([P, PAIR, F_OUT], F32, name="gate")
+            nc.scalar.activation(out=gate[:], in_=acc_tiles[j][:, :, 0:F_OUT], func=SILU)
+            gate_tiles[j] = gate
+
+        def gate_product(j):
+            g, half_group = (j * PAIR) // GROUP, (j * PAIR) % GROUP
+            if half_group == 0:
+                out_tiles[g] = result_pool.tile([P, GROUP, F_OUT], F32, name="out_sb")
             nc.vector.tensor_tensor(
-                out=out_tiles[g][:, t * F_OUT : (t + 1) * F_OUT],
-                in0=gate[:],
-                in1=acc[:, F_OUT : 2 * F_OUT],
+                out=out_tiles[g][:, half_group : half_group + PAIR, :],
+                in0=gate_tiles[j][:],
+                in1=acc_tiles[j][:, :, F_OUT : 2 * F_OUT],
                 op=MULT,
             )
-            if t == GROUP - 1:
-                nc.sync.dma_start(out=out_view[g], in_=out_tiles[g][:])
 
+        def store(g):
+            nc.sync.dma_start(out=out_view[g], in_=out_tiles[g][:].rearrange("p t f -> p (t f)"))
+
+        n_steps = n_tiles // PAIR
+        pairs_in_group = GROUP // PAIR
         sort_words(0)
-        for step in range(n_tiles + LAG_MATMUL):
-            if step + PREFETCH < n_tiles:
-                x_tiles[step + PREFETCH] = load(step + PREFETCH)
-            if step + 1 < n_tiles:
-                sort_words(step + 1)
-            if step < 2:
-                quantise_weights(step)
-            if 0 <= step - LAG_QUANTISE < n_tiles:
-                quantise(step - LAG_QUANTISE)
-            if step < n_tiles:
-                transpose_and_regroup(step)
-            if step >= LAG_MATMUL:
-                multiply_and_gate(step - LAG_MATMUL)
+        for j in range(n_steps + 2):
+            gated = j - 2
+            if gated >= 1 and gated % pairs_in_group == 0:
+                store(gated // pairs_in_group - 1)
+            if 1 <= j < n_steps:
+                for r in range(j * PAIR + X_BUFS - PAIR, j * PAIR + X_BUFS):
+                    if r < n_tiles:
+                        x_tiles[r] = load(r)
+            if gated >= 0:
+                silu(gated)
+            for h in range(PAIR):
+                r = j * PAIR + h
+                if r + 1 < n_tiles:
+                    sort_words(r + 1)
+                if h == 0 and gated >= 0:
+                    gate_product(gated)
+                if j == 0:
+                    quantise_weights(h)
+                if 1 <= r <= n_tiles:
+                    quantise(r - 1)
+                if r < n_tiles:
+                    transpose_and_regroup(r, (BANKS - 1,) if h == 0 else ())
+            if 1 <= j <= n_steps:
+                multiply(j - 1)
+        store(groups - 1)

@@ -25,7 +25,7 @@ FLOPS = 2 * 4096 * 4096 * SIDES * F_OUT
 
 X_BUFS = 8
 PAIR = 2
-T_BANKS = 7
+T_BANKS = 6
 BANK_COMPS = 2
 BANKS = UNITS // BANK_COMPS
 QUARTERS = 4
@@ -62,7 +62,7 @@ def tile_swiglumlp_pa_t_kernel(tc, x, wq_gate, wq_up, out):
         codes_pool = ctx.enter_context(tc.tile_pool(name="codes_pool", bufs=4))
         result_pool = ctx.enter_context(tc.tile_pool(name="result_pool", bufs=3))
         psum_t = ctx.enter_context(tc.psum_pool(name="psum_t", bufs=T_BANKS))
-        psum_acc = ctx.enter_context(tc.psum_pool(name="psum_acc", bufs=1))
+        psum_acc = ctx.enter_context(tc.psum_pool(name="psum_acc", bufs=2))
         ctx.enter_context(tc.manual_schedule())
 
         def load(r):
@@ -169,10 +169,10 @@ def tile_swiglumlp_pa_t_kernel(tc, x, wq_gate, wq_up, out):
             )
             code_tiles[r] = (codes, scales)
 
-        def multiply(j):
+        def multiply(tiles):
             acc = psum_acc.tile([P, PAIR, n_cols], F32, name="acc")
-            for h in range(PAIR):
-                codes, scales = code_tiles[j * PAIR + h]
+            for h, r in enumerate(tiles):
+                codes, scales = code_tiles[r]
                 for i in range(UNITS):
                     nc.tensor.matmul_mx(
                         out=acc[:, h, :],
@@ -183,52 +183,67 @@ def tile_swiglumlp_pa_t_kernel(tc, x, wq_gate, wq_up, out):
                         start=(i == 0),
                         stop=(i == UNITS - 1),
                     )
-            acc_tiles[j] = acc
+            acc_tiles[tiles[0]] = acc
 
-        def silu(j):
+        def silu(tiles):
+            n = len(tiles)
             gate = result_pool.tile([P, PAIR, F_OUT], F32, name="gate")
-            nc.scalar.activation(out=gate[:], in_=acc_tiles[j][:, :, 0:F_OUT], func=SILU)
-            gate_tiles[j] = gate
+            nc.scalar.activation(out=gate[:, 0:n, :], in_=acc_tiles[tiles[0]][:, 0:n, 0:F_OUT], func=SILU)
+            gate_tiles[tiles[0]] = gate
 
-        def gate_product(j):
-            g, half_group = (j * PAIR) // GROUP, (j * PAIR) % GROUP
-            if half_group == 0:
+        def gate_product(tiles):
+            n = len(tiles)
+            g, t = tiles[0] // GROUP, tiles[0] % GROUP
+            if t == 0:
                 out_tiles[g] = result_pool.tile([P, GROUP, F_OUT], F32, name="out_sb")
             nc.vector.tensor_tensor(
-                out=out_tiles[g][:, half_group : half_group + PAIR, :],
-                in0=gate_tiles[j][:],
-                in1=acc_tiles[j][:, :, F_OUT : 2 * F_OUT],
+                out=out_tiles[g][:, t : t + n, :],
+                in0=gate_tiles[tiles[0]][:, 0:n, :],
+                in1=acc_tiles[tiles[0]][:, 0:n, F_OUT : 2 * F_OUT],
                 op=MULT,
             )
 
-        def store(g):
-            nc.sync.dma_start(out=out_view[g], in_=out_tiles[g][:].rearrange("p t f -> p (t f)"))
+        def store(g, first, count):
+            nc.sync.dma_start(
+                out=out_view[g][:, first * F_OUT : (first + count) * F_OUT],
+                in_=out_tiles[g][:, first : first + count, :].rearrange("p t f -> p (t f)"),
+            )
+
+        def pair(j):
+            return [j * PAIR, j * PAIR + 1]
 
         n_steps = n_tiles // PAIR
         pairs_in_group = GROUP // PAIR
         sort_words(0)
-        for j in range(n_steps + 2):
+        for j in range(n_steps + 1):
             gated = j - 2
             if gated >= 1 and gated % pairs_in_group == 0:
-                store(gated // pairs_in_group - 1)
+                store(gated // pairs_in_group - 1, 0, GROUP)
             if 1 <= j < n_steps:
                 for r in range(j * PAIR + X_BUFS - PAIR, j * PAIR + X_BUFS):
                     if r < n_tiles:
                         x_tiles[r] = load(r)
             if gated >= 0:
-                silu(gated)
+                silu(pair(gated))
             for h in range(PAIR):
                 r = j * PAIR + h
                 if r + 1 < n_tiles:
                     sort_words(r + 1)
-                if h == 0 and gated >= 0:
-                    gate_product(gated)
                 if j == 0:
                     quantise_weights(h)
                 if 1 <= r <= n_tiles:
                     quantise(r - 1)
+                if h == 0 and gated >= 0:
+                    gate_product(pair(gated))
                 if r < n_tiles:
                     transpose_and_regroup(r, (BANKS - 1,) if h == 0 else ())
-            if 1 <= j <= n_steps:
-                multiply(j - 1)
-        store(groups - 1)
+            if 1 <= j < n_steps:
+                multiply(pair(j - 1))
+        for r in pair(n_steps - 1):
+            multiply([r])
+        for r in pair(n_steps - 1):
+            silu([r])
+            gate_product([r])
+            if r == n_tiles - 2:
+                store(groups - 1, 0, GROUP - 1)
+        store(groups - 1, GROUP - 1, 1)

@@ -30,6 +30,7 @@ BANK_COMPS = 2
 BANKS = UNITS // BANK_COMPS
 QUARTERS = 4
 QUARTER = 64
+LOWS = 4
 
 
 def octonion_table():
@@ -95,19 +96,44 @@ def tile_swiglumlp_pa_t_kernel(tc, x, wq_gate, wq_up, out):
             )
         w_grouped = const.tile([P, UNITS * SIDES * F_OUT * PACK], BF16, name="w_grouped", align_bytes=64)
         w_grouped_words = w_grouped[:].bitcast(F32).rearrange(
-            "p (i s c u) -> p i s c u", i=UNITS, s=SIDES, u=2
+            "p (i j s o u) -> p i j s o u", i=UNITS, j=UNITS, s=SIDES, u=2
         )
-        nc.vector.tensor_copy(out=w_grouped_words[:, 0], in_=wt[:].rearrange("p s u c -> p s c u"))
-        w_blocks = w_grouped[:].rearrange("p (i s k e) -> p i s k e", i=UNITS, s=SIDES, k=UNITS)
-        for i in range(1, UNITS):
-            for k in range(UNITS):
-                j, sign = table[(i, k)]
-                if i % 3 == 1:
-                    nc.scalar.mul(w_blocks[:, i, :, k, :], w_blocks[:, 0, :, j, :], sign)
-                else:
-                    nc.vector.tensor_scalar_mul(
-                        out=w_blocks[:, i, :, k, :], in0=w_blocks[:, 0, :, j, :], scalar1=sign
+        nc.scalar.copy(out=w_grouped_words[:, 0, :, 0], in_=wt[:, 0].rearrange("p u (j o) -> p j o u", j=UNITS))
+        nc.vector.tensor_copy(out=w_grouped_words[:, 0, :, 1], in_=wt[:, 1].rearrange("p u (j o) -> p j o u", j=UNITS))
+        w_blocks = w_grouped[:].rearrange("p (i h l c) -> p i h l c", i=UNITS, h=2, l=LOWS)
+
+        def run(values):
+            step = values[1] - values[0]
+            assert all(b - a == step for a, b in zip(values, values[1:]))
+            stop = values[-1] + (1 if step > 0 else -1)
+            return slice(values[0], stop if stop >= 0 else None, step)
+
+        def expand(i, scale_and_copy):
+            upper, lower = i // LOWS, i % LOWS
+            for sign in (1.0, -1.0):
+                lows = [[l for l in range(LOWS) if table[(i, h * LOWS + l)][1] == sign] for h in range(2)]
+                if lows[0] == lows[1]:
+                    scale_and_copy(
+                        w_blocks[:, i, :, run(lows[0]), :],
+                        w_blocks[:, 0, run([upper, 1 - upper]), run([l ^ lower for l in lows[0]]), :],
+                        sign,
                     )
+                else:
+                    for h in range(2):
+                        if lows[h]:
+                            scale_and_copy(
+                                w_blocks[:, i, h, run(lows[h]), :],
+                                w_blocks[:, 0, h ^ upper, run([l ^ lower for l in lows[h]]), :],
+                                sign,
+                            )
+
+        def on_vector(dst, src, sign):
+            nc.vector.tensor_scalar_mul(out=dst, in0=src, scalar1=sign)
+
+        def on_scalar(dst, src, sign):
+            nc.scalar.mul(dst, src, sign)
+
+        expand(1, on_scalar)
         n_cols = SIDES * F_OUT
         w_codes = const.tile([P, UNITS * n_cols], U32, name="w_codes", align_bytes=64)
         w_scales = const.tile([P, UNITS * n_cols], U8, name="w_scales", align_bytes=64)
@@ -185,10 +211,17 @@ def tile_swiglumlp_pa_t_kernel(tc, x, wq_gate, wq_up, out):
                     )
             acc_tiles[tiles[0]] = acc
 
+        def by_side(first_tile):
+            return acc_tiles[first_tile][:].rearrange("p t (k s o) -> p t k s o", k=UNITS, s=SIDES)
+
         def silu(tiles):
             n = len(tiles)
             gate = result_pool.tile([P, PAIR, F_OUT], F32, name="gate")
-            nc.scalar.activation(out=gate[:, 0:n, :], in_=acc_tiles[tiles[0]][:, 0:n, 0:F_OUT], func=SILU)
+            nc.scalar.activation(
+                out=gate[:, 0:n, :].rearrange("p t (k o) -> p t k o", k=UNITS),
+                in_=by_side(tiles[0])[:, 0:n, :, 0, :],
+                func=SILU,
+            )
             gate_tiles[tiles[0]] = gate
 
         def gate_product(tiles):
@@ -197,9 +230,9 @@ def tile_swiglumlp_pa_t_kernel(tc, x, wq_gate, wq_up, out):
             if t == 0:
                 out_tiles[g] = result_pool.tile([P, GROUP, F_OUT], F32, name="out_sb")
             nc.vector.tensor_tensor(
-                out=out_tiles[g][:, t : t + n, :],
-                in0=gate_tiles[tiles[0]][:, 0:n, :],
-                in1=acc_tiles[tiles[0]][:, 0:n, F_OUT : 2 * F_OUT],
+                out=out_tiles[g][:, t : t + n, :].rearrange("p t (k o) -> p t k o", k=UNITS),
+                in0=gate_tiles[tiles[0]][:, 0:n, :].rearrange("p t (k o) -> p t k o", k=UNITS),
+                in1=by_side(tiles[0])[:, 0:n, :, 1, :],
                 op=MULT,
             )
 
@@ -214,7 +247,11 @@ def tile_swiglumlp_pa_t_kernel(tc, x, wq_gate, wq_up, out):
 
         n_steps = n_tiles // PAIR
         pairs_in_group = GROUP // PAIR
+        expand(2, on_vector)
+        expand(3, on_vector)
         sort_words(0)
+        expand(4, on_vector)
+        expand(5, on_vector)
         for j in range(n_steps + 1):
             gated = j - 2
             if gated >= 1 and gated % pairs_in_group == 0:
@@ -227,16 +264,21 @@ def tile_swiglumlp_pa_t_kernel(tc, x, wq_gate, wq_up, out):
                 silu(pair(gated))
             for h in range(PAIR):
                 r = j * PAIR + h
+                if r == 1:
+                    expand(6, on_vector)
+                    expand(7, on_vector)
                 if r + 1 < n_tiles:
                     sort_words(r + 1)
                 if j == 0:
                     quantise_weights(h)
-                if 1 <= r <= n_tiles:
+                if r == 2:
+                    quantise(0)
+                if 2 <= r <= n_tiles:
                     quantise(r - 1)
                 if h == 0 and gated >= 0:
                     gate_product(pair(gated))
                 if r < n_tiles:
-                    transpose_and_regroup(r, (BANKS - 1,) if h == 0 else ())
+                    transpose_and_regroup(r, (BANKS - 1,) if h == 0 and j >= 2 else ())
             if 1 <= j < n_steps:
                 multiply(pair(j - 1))
         for r in pair(n_steps - 1):

@@ -260,8 +260,6 @@ def tile_swiglumlp_pa_t_kernel(tc, x, wq_gate, wq_up, out):
                 for r in range(j * PAIR + X_BUFS - PAIR, j * PAIR + X_BUFS):
                     if r < n_tiles:
                         x_tiles[r] = load(r)
-            if gated >= 0:
-                silu(pair(gated))
             for h in range(PAIR):
                 r = j * PAIR + h
                 if r == 1:
@@ -275,10 +273,11 @@ def tile_swiglumlp_pa_t_kernel(tc, x, wq_gate, wq_up, out):
                     quantise(0)
                 if 2 <= r <= n_tiles:
                     quantise(r - 1)
-                if h == 0 and gated >= 0:
-                    gate_product(pair(gated))
                 if r < n_tiles:
                     transpose_and_regroup(r, (BANKS - 1,) if h == 0 and j >= 2 else ())
+                if h == 0 and gated >= 0:
+                    silu(pair(gated))
+                    gate_product(pair(gated))
             if 1 <= j < n_steps:
                 multiply(pair(j - 1))
         for r in pair(n_steps - 1):

@@ -134,6 +134,7 @@ def tile_swiglumlp_pa_t_kernel(tc, x, wq_gate, wq_up, out):
             nc.scalar.mul(dst, src, sign)
 
         expand(1, on_scalar)
+        expand(4, on_scalar)
         n_cols = SIDES * F_OUT
         w_codes = const.tile([P, UNITS * n_cols], U32, name="w_codes", align_bytes=64)
         w_scales = const.tile([P, UNITS * n_cols], U8, name="w_scales", align_bytes=64)
@@ -250,7 +251,6 @@ def tile_swiglumlp_pa_t_kernel(tc, x, wq_gate, wq_up, out):
         expand(2, on_vector)
         expand(3, on_vector)
         sort_words(0)
-        expand(4, on_vector)
         expand(5, on_vector)
         for j in range(n_steps + 1):
             gated = j - 2

@@ -23,7 +23,7 @@ TRIPLES = [(1, 2, 3), (1, 4, 5), (1, 7, 6), (2, 4, 6), (2, 5, 7), (3, 4, 7), (3,
 
 FLOPS = 2 * 4096 * 4096 * SIDES * F_OUT
 
-X_BUFS = 8
+X_BUFS = 9
 PAIR = 2
 T_BANKS = 6
 BANK_COMPS = 2
@@ -58,10 +58,10 @@ def tile_swiglumlp_pa_t_kernel(tc, x, wq_gate, wq_up, out):
     with ExitStack() as ctx:
         const = ctx.enter_context(tc.tile_pool(name="const", bufs=1))
         x_pool = ctx.enter_context(tc.tile_pool(name="x_pool", bufs=X_BUFS))
-        sorted_pool = ctx.enter_context(tc.tile_pool(name="sorted_pool", bufs=4))
-        grouped_pool = ctx.enter_context(tc.tile_pool(name="grouped_pool", bufs=4))
-        codes_pool = ctx.enter_context(tc.tile_pool(name="codes_pool", bufs=4))
-        result_pool = ctx.enter_context(tc.tile_pool(name="result_pool", bufs=3))
+        sorted_pool = ctx.enter_context(tc.tile_pool(name="sorted_pool", bufs=5))
+        grouped_pool = ctx.enter_context(tc.tile_pool(name="grouped_pool", bufs=6))
+        codes_pool = ctx.enter_context(tc.tile_pool(name="codes_pool", bufs=8))
+        result_pool = ctx.enter_context(tc.tile_pool(name="result_pool", bufs=4))
         psum_t = ctx.enter_context(tc.psum_pool(name="psum_t", bufs=T_BANKS))
         psum_acc = ctx.enter_context(tc.psum_pool(name="psum_acc", bufs=2))
         ctx.enter_context(tc.manual_schedule())
@@ -196,44 +196,47 @@ def tile_swiglumlp_pa_t_kernel(tc, x, wq_gate, wq_up, out):
             )
             code_tiles[r] = (codes, scales)
 
-        def multiply(tiles):
-            acc = psum_acc.tile([P, PAIR, n_cols], F32, name="acc")
-            for h, r in enumerate(tiles):
-                codes, scales = code_tiles[r]
-                for i in range(UNITS):
-                    nc.tensor.matmul_mx(
-                        out=acc[:, h, :],
-                        lhsT=codes[:, i * P : (i + 1) * P].bitcast(FP8X4),
-                        lhsT_scale=scales[:, i * P : (i + 1) * P],
-                        rhs=w_codes[:, i * n_cols : (i + 1) * n_cols].bitcast(FP8X4),
-                        rhs_scale=w_scales[:, i * n_cols : (i + 1) * n_cols],
-                        start=(i == 0),
-                        stop=(i == UNITS - 1),
-                    )
-            acc_tiles[tiles[0]] = acc
+        def multiply(r, bank=None):
+            if bank is None:
+                if r % PAIR == 0 or r - 1 not in acc_tiles:
+                    bank = psum_acc.tile([P, PAIR, n_cols], F32, name="acc")
+                else:
+                    bank = acc_tiles[r - 1]
+            acc_tiles[r] = bank
+            codes, scales = code_tiles[r]
+            for i in range(UNITS):
+                nc.tensor.matmul_mx(
+                    out=bank[:, r % PAIR, :],
+                    lhsT=codes[:, i * P : (i + 1) * P].bitcast(FP8X4),
+                    lhsT_scale=scales[:, i * P : (i + 1) * P],
+                    rhs=w_codes[:, i * n_cols : (i + 1) * n_cols].bitcast(FP8X4),
+                    rhs_scale=w_scales[:, i * n_cols : (i + 1) * n_cols],
+                    start=(i == 0),
+                    stop=(i == UNITS - 1),
+                )
 
-        def by_side(first_tile):
-            return acc_tiles[first_tile][:].rearrange("p t (k s o) -> p t k s o", k=UNITS, s=SIDES)
+        def by_side(r):
+            return acc_tiles[r][:].rearrange("p t (k s o) -> p t k s o", k=UNITS, s=SIDES)
 
         def silu(tiles):
-            n = len(tiles)
+            t, n = tiles[0] % PAIR, len(tiles)
             gate = result_pool.tile([P, PAIR, F_OUT], F32, name="gate")
             nc.scalar.activation(
                 out=gate[:, 0:n, :].rearrange("p t (k o) -> p t k o", k=UNITS),
-                in_=by_side(tiles[0])[:, 0:n, :, 0, :],
+                in_=by_side(tiles[0])[:, t : t + n, :, 0, :],
                 func=SILU,
             )
             gate_tiles[tiles[0]] = gate
 
         def gate_product(tiles):
-            n = len(tiles)
+            h, n = tiles[0] % PAIR, len(tiles)
             g, t = tiles[0] // GROUP, tiles[0] % GROUP
             if t == 0:
                 out_tiles[g] = result_pool.tile([P, GROUP, F_OUT], F32, name="out_sb")
             nc.vector.tensor_tensor(
                 out=out_tiles[g][:, t : t + n, :].rearrange("p t (k o) -> p t k o", k=UNITS),
                 in0=gate_tiles[tiles[0]][:, 0:n, :].rearrange("p t (k o) -> p t k o", k=UNITS),
-                in1=by_side(tiles[0])[:, 0:n, :, 1, :],
+                in1=by_side(tiles[0])[:, h : h + n, :, 1, :],
                 op=MULT,
             )
 
@@ -243,46 +246,91 @@ def tile_swiglumlp_pa_t_kernel(tc, x, wq_gate, wq_up, out):
                 in_=out_tiles[g][:, first : first + count, :].rearrange("p t f -> p (t f)"),
             )
 
-        def pair(j):
-            return [j * PAIR, j * PAIR + 1]
+        def sort_to(last):
+            for r in range(len(sorted_tiles), min(last, n_tiles - 1) + 1):
+                sort_words(r)
 
-        n_steps = n_tiles // PAIR
-        pairs_in_group = GROUP // PAIR
+        def quantise_to(last):
+            for r in range(len(code_tiles), last + 1):
+                quantise(r)
+
+        def gate_to(end):
+            parts = []
+            r = progress["gated"]
+            while r < end:
+                n = PAIR if r % PAIR == 0 and r + 1 < end else 1
+                parts.append(list(range(r, r + n)))
+                r += n
+            progress["gated"] = end
+            for tiles in parts:
+                silu(tiles)
+            for tiles in parts:
+                gate_product(tiles)
+
+        def start_run(a):
+            while (progress["stored"] + 1) * GROUP <= progress["gated"]:
+                store(progress["stored"], 0, GROUP)
+                progress["stored"] += 1
+            if a > 0:
+                for r in range(len(x_tiles), min(a + X_BUFS, n_tiles)):
+                    x_tiles[r] = load(r)
+
+        def multiply_to(end):
+            for r in range(progress["multiplied"], end):
+                multiply(r)
+            progress["multiplied"] = end
+
+        def pair_run(a):
+            multiplied = progress["multiplied"]
+            start_run(a)
+            for r in (a, a + 1):
+                if r == 1:
+                    expand(6, on_vector)
+                    expand(7, on_vector)
+                sort_to(r + 1)
+                if a == 0:
+                    quantise_weights(r)
+                if r >= 2:
+                    quantise_to(r - 1)
+                transpose_and_regroup(r, (BANKS - 1,) if r == a and a >= 4 else ())
+                if r == a:
+                    gate_to(multiplied)
+
+        def triple_run(a):
+            multiplied = progress["multiplied"]
+            start_run(a)
+            gate_to(multiplied)
+            sort_to(a + 1)
+            transpose_and_regroup(a, (2,))
+            sort_to(a + 2)
+            quantise_to(a - 1)
+            transpose_and_regroup(a + 1, ())
+            quantise_to(a)
+            transpose_and_regroup(a + 2, (3,))
+            sort_to(a + 3)
+            quantise_to(a + 1)
+            sort_to(a + 4)
+
+        progress = {"multiplied": 0, "gated": 0, "stored": 0}
         expand(2, on_vector)
         expand(3, on_vector)
         sort_words(0)
         expand(5, on_vector)
-        for j in range(n_steps + 1):
-            gated = j - 2
-            if gated >= 1 and gated % pairs_in_group == 0:
-                store(gated // pairs_in_group - 1, 0, GROUP)
-            if 1 <= j < n_steps:
-                for r in range(j * PAIR + X_BUFS - PAIR, j * PAIR + X_BUFS):
-                    if r < n_tiles:
-                        x_tiles[r] = load(r)
-            for h in range(PAIR):
-                r = j * PAIR + h
-                if r == 1:
-                    expand(6, on_vector)
-                    expand(7, on_vector)
-                if r + 1 < n_tiles:
-                    sort_words(r + 1)
-                if j == 0:
-                    quantise_weights(h)
-                if r == 2:
-                    quantise(0)
-                if 2 <= r <= n_tiles:
-                    quantise(r - 1)
-                if r < n_tiles:
-                    transpose_and_regroup(r, (BANKS - 1,) if h == 0 and j >= 2 else ())
-                if h == 0 and gated >= 0:
-                    silu(pair(gated))
-                    gate_product(pair(gated))
-            if 1 <= j < n_steps:
-                multiply(pair(j - 1))
-        for r in pair(n_steps - 1):
-            multiply([r])
-        for r in pair(n_steps - 1):
+        a = 0
+        for n in [2] * 3 + [3] * 8 + [2]:
+            (pair_run if n == 2 else triple_run)(a)
+            if a > 0:
+                multiply_to(a)
+            if a == 4:
+                sort_to(7)
+            a += n
+        last = n_tiles - PAIR
+        quantise_to(n_tiles - 1)
+        gate_to(last)
+        for r in range(last, n_tiles):
+            multiply(r, psum_t.tile([P, PAIR, n_cols], F32, name="xt"))
+        start_run(0)
+        for r in range(last, n_tiles):
             silu([r])
             gate_product([r])
             if r == n_tiles - 2:

@@ -58,10 +58,10 @@ def tile_swiglumlp_pa_t_kernel(tc, x, wq_gate, wq_up, out):
     with ExitStack() as ctx:
         const = ctx.enter_context(tc.tile_pool(name="const", bufs=1))
         x_pool = ctx.enter_context(tc.tile_pool(name="x_pool", bufs=X_BUFS))
-        sorted_pool = ctx.enter_context(tc.tile_pool(name="sorted_pool", bufs=5))
-        grouped_pool = ctx.enter_context(tc.tile_pool(name="grouped_pool", bufs=6))
-        codes_pool = ctx.enter_context(tc.tile_pool(name="codes_pool", bufs=8))
-        result_pool = ctx.enter_context(tc.tile_pool(name="result_pool", bufs=4))
+        sorted_pool = ctx.enter_context(tc.tile_pool(name="sorted_pool", bufs=6))
+        grouped_pool = ctx.enter_context(tc.tile_pool(name="grouped_pool", bufs=5))
+        codes_pool = ctx.enter_context(tc.tile_pool(name="codes_pool", bufs=7))
+        result_pool = ctx.enter_context(tc.tile_pool(name="result_pool", bufs=3))
         psum_t = ctx.enter_context(tc.psum_pool(name="psum_t", bufs=T_BANKS))
         psum_acc = ctx.enter_context(tc.psum_pool(name="psum_acc", bufs=2))
         ctx.enter_context(tc.manual_schedule())
@@ -148,6 +148,7 @@ def tile_swiglumlp_pa_t_kernel(tc, x, wq_gate, wq_up, out):
             )
 
         sorted_tiles = {}
+        turned_tiles = {}
         grouped_tiles = {}
         code_tiles = {}
         acc_tiles = {}
@@ -164,11 +165,9 @@ def tile_swiglumlp_pa_t_kernel(tc, x, wq_gate, wq_up, out):
             )
             sorted_tiles[r] = sorted_words
 
-        def transpose_and_regroup(r, vector_banks):
+        def turn(r):
             outer = sorted_tiles[r]
             inner = x_tiles[r][:].bitcast(F32)
-            grouped = grouped_pool.tile([P, features], BF16, name="grouped", align_bytes=64)
-            grouped_words = grouped[:].bitcast(F32).rearrange("p (c r u) -> p c r u", c=UNITS, u=2)
             banks = []
             for b in range(BANKS):
                 xt = psum_t.tile([P, BANK_COMPS, 2, P], F32, name="xt")
@@ -179,14 +178,21 @@ def tile_swiglumlp_pa_t_kernel(tc, x, wq_gate, wq_up, out):
                         xt[:, c, 1, :], inner[:, comp * 2 * P + QUARTER : comp * 2 * P + 3 * QUARTER], ident[:]
                     )
                 banks.append(xt)
-            for b in range(BANKS):
-                dst = grouped_words[:, b * BANK_COMPS : (b + 1) * BANK_COMPS]
-                src = banks[b][:].rearrange("p c u r -> p c r u")
-                if b in vector_banks:
-                    nc.vector.tensor_copy(out=dst, in_=src)
-                else:
-                    nc.scalar.copy(out=dst, in_=src)
+            turned_tiles[r] = banks
+            grouped = grouped_pool.tile([P, features], BF16, name="grouped", align_bytes=64)
             grouped_tiles[r] = grouped
+
+        def regroup(r, bank, copy):
+            words = grouped_tiles[r][:].bitcast(F32).rearrange("p (c r u) -> p c r u", c=UNITS, u=2)
+            copy(
+                out=words[:, bank * BANK_COMPS : (bank + 1) * BANK_COMPS],
+                in_=turned_tiles[r][bank][:].rearrange("p c u r -> p c r u"),
+            )
+
+        def transpose_and_regroup(r, vector_banks):
+            turn(r)
+            for b in range(BANKS):
+                regroup(r, b, nc.vector.tensor_copy if b in vector_banks else nc.scalar.copy)
 
         def quantise(r):
             codes = codes_pool.tile([P, UNITS * P], U32, name="codes", align_bytes=64)
@@ -198,7 +204,7 @@ def tile_swiglumlp_pa_t_kernel(tc, x, wq_gate, wq_up, out):
 
         def multiply(r, bank=None):
             if bank is None:
-                if r % PAIR == 0 or r - 1 not in acc_tiles:
+                if r % PAIR == 0 or r in firsts:
                     bank = psum_acc.tile([P, PAIR, n_cols], F32, name="acc")
                 else:
                     bank = acc_tiles[r - 1]
@@ -254,14 +260,18 @@ def tile_swiglumlp_pa_t_kernel(tc, x, wq_gate, wq_up, out):
             for r in range(len(code_tiles), last + 1):
                 quantise(r)
 
-        def gate_to(end):
+        def parts_to(end):
             parts = []
             r = progress["gated"]
             while r < end:
-                n = PAIR if r % PAIR == 0 and r + 1 < end else 1
+                n = PAIR if r % PAIR == 0 and r + 1 < end and r + 1 not in firsts else 1
                 parts.append(list(range(r, r + n)))
                 r += n
             progress["gated"] = end
+            return parts
+
+        def gate_to(end):
+            parts = parts_to(end)
             for tiles in parts:
                 silu(tiles)
             for tiles in parts:
@@ -292,37 +302,54 @@ def tile_swiglumlp_pa_t_kernel(tc, x, wq_gate, wq_up, out):
                     quantise_weights(r)
                 if r >= 2:
                     quantise_to(r - 1)
+                if r == n_tiles - PAIR:
+                    gate_to(multiplied)
                 transpose_and_regroup(r, (BANKS - 1,) if r == a and a >= 4 else ())
                 if r == a:
                     gate_to(multiplied)
 
         def triple_run(a):
-            multiplied = progress["multiplied"]
+            on_act, on_dve = nc.scalar.copy, nc.vector.tensor_copy
             start_run(a)
-            gate_to(multiplied)
+            parts = parts_to(progress["multiplied"])
             sort_to(a + 1)
-            transpose_and_regroup(a, (2,))
+            for tiles in parts:
+                silu(tiles)
+            for tiles in parts:
+                gate_product(tiles)
+            turn(a)
+            regroup(a, 0, on_act)
+            regroup(a, 1, on_dve)
+            regroup(a, 2, on_act)
+            regroup(a, 3, on_dve)
             sort_to(a + 2)
+            turn(a + 1)
+            for b in range(BANKS):
+                regroup(a + 1, b, on_act)
             quantise_to(a - 1)
-            transpose_and_regroup(a + 1, ())
+            turn(a + 2)
+            for b in range(BANKS):
+                regroup(a + 2, b, on_act)
             quantise_to(a)
-            transpose_and_regroup(a + 2, (3,))
             sort_to(a + 3)
             quantise_to(a + 1)
-            sort_to(a + 4)
+            sort_to(a + (5))
 
+        firsts = list(range(0, 12, 2)) + list(range(12, 30, 3)) + [30]
         progress = {"multiplied": 0, "gated": 0, "stored": 0}
         expand(2, on_vector)
         expand(3, on_vector)
         sort_words(0)
         expand(5, on_vector)
         a = 0
-        for n in [2] * 3 + [3] * 8 + [2]:
+        for n in [2] * 6 + [3] * 6 + [2]:
             (pair_run if n == 2 else triple_run)(a)
             if a > 0:
                 multiply_to(a)
-            if a == 4:
-                sort_to(7)
+            if a == 8:
+                sort_to(11)
+            if a == 10:
+                sort_to(14)
             a += n
         last = n_tiles - PAIR
         quantise_to(n_tiles - 1)

from contextlib import ExitStack

import concourse.mybir as mybir
from concourse.masks import make_identity

F32 = mybir.dt.float32
BF16 = mybir.dt.bfloat16
U32 = mybir.dt.uint32
U8 = mybir.dt.uint8
FP8X4 = mybir.dt.float8_e4m3fn_x4
SILU = mybir.ActivationFunctionType.Silu
MULT = mybir.AluOpType.mult

P = 128
PACK = 4
UNITS = 8
COMP = 512
O16 = 16
F_OUT = UNITS * O16
SIDES = 2
GROUP = 4
TRIPLES = [(1, 2, 3), (1, 4, 5), (1, 7, 6), (2, 4, 6), (2, 5, 7), (3, 4, 7), (3, 6, 5)]

FLOPS = 2 * 4096 * 4096 * SIDES * F_OUT

X_BUFS = 9
PAIR = 2
T_BANKS = 6
BANK_COMPS = 2
BANKS = UNITS // BANK_COMPS
QUARTERS = 4
QUARTER = 64
LOWS = 4


def octonion_table():
    table = {(0, 0): (0, 1.0)}
    for i in range(1, UNITS):
        table[(i, i)] = (0, 1.0)
        table[(0, i)] = (i, 1.0)
        table[(i, 0)] = (i, -1.0)
    for a, b, c in TRIPLES:
        for p, q, r in ((a, b, c), (b, c, a), (c, a, b)):
            table[(q, r)] = (p, 1.0)
            table[(p, r)] = (q, -1.0)
    return table


def tile_swiglumlp_pa_t_kernel(tc, x, wq_gate, wq_up, out):
    nc = tc.nc
    groups = x.shape[0]
    n_tiles = groups * GROUP
    features = UNITS * COMP
    x_view = x.rearrange("g (p t) k -> g t p k", t=GROUP)
    out_view = out.rearrange("g (p t) f -> g p (t f)", t=GROUP)
    table = octonion_table()

    with ExitStack() as ctx:
        const = ctx.enter_context(tc.tile_pool(name="const", bufs=1))
        x_pool = ctx.enter_context(tc.tile_pool(name="x_pool", bufs=X_BUFS))
        sorted_pool = ctx.enter_context(tc.tile_pool(name="sorted_pool", bufs=6))
        grouped_pool = ctx.enter_context(tc.tile_pool(name="grouped_pool", bufs=5))
        codes_pool = ctx.enter_context(tc.tile_pool(name="codes_pool", bufs=7))
        result_pool = ctx.enter_context(tc.tile_pool(name="result_pool", bufs=3))
        psum_t = ctx.enter_context(tc.psum_pool(name="psum_t", bufs=T_BANKS))
        psum_acc = ctx.enter_context(tc.psum_pool(name="psum_acc", bufs=2))
        ctx.enter_context(tc.manual_schedule())

        def load(r):
            x_sb = x_pool.tile([P, features], BF16, name="x_sb")
            nc.sync.dma_start(out=x_sb[:], in_=x_view[r // GROUP, r % GROUP])
            return x_sb

        w_raw = const.tile([P, SIDES * COMP], BF16, name="w_raw")
        nc.sync.dma_start(out=w_raw[:, 0:COMP], in_=wq_gate.rearrange("j o d -> (j o) d"))
        nc.sync.dma_start(out=w_raw[:, COMP : 2 * COMP], in_=wq_up.rearrange("j o d -> (j o) d"))
        x_tiles = {}
        for r in range(X_BUFS):
            x_tiles[r] = load(r)

        ident = const.tile([P, P], F32, name="ident")
        make_identity(nc, ident[:])
        warm = const.tile([P, 1], F32, name="warm")
        nc.vector.memset(warm[:], 0.0)
        nc.scalar.activation(out=warm[:], in_=warm[:], func=SILU)

        w_words = w_raw[:].bitcast(F32).rearrange("p (s q w) -> p s q w", s=SIDES, q=QUARTERS)
        w_outer = const.tile([P, SIDES, 2, QUARTER], F32, name="w_outer")
        nc.vector.tensor_copy(out=w_outer[:], in_=w_words[:, :, 0 : QUARTERS : QUARTERS - 1, :])
        w_flat = w_raw[:].bitcast(F32)
        wt = psum_t.tile([P, SIDES, 2, P], F32, name="xt")
        for s in range(SIDES):
            nc.tensor.transpose(wt[:, s, 0, :], w_outer[:, s].rearrange("p h w -> p (h w)"), ident[:])
            nc.tensor.transpose(
                wt[:, s, 1, :], w_flat[:, s * 2 * P + QUARTER : s * 2 * P + 3 * QUARTER], ident[:]
            )
        w_grouped = const.tile([P, UNITS * SIDES * F_OUT * PACK], BF16, name="w_grouped", align_bytes=64)
        w_grouped_words = w_grouped[:].bitcast(F32).rearrange(
            "p (i j s o u) -> p i j s o u", i=UNITS, j=UNITS, s=SIDES, u=2
        )
        nc.scalar.copy(out=w_grouped_words[:, 0, :, 0], in_=wt[:, 0].rearrange("p u (j o) -> p j o u", j=UNITS))
        nc.vector.tensor_copy(out=w_grouped_words[:, 0, :, 1], in_=wt[:, 1].rearrange("p u (j o) -> p j o u", j=UNITS))
        w_blocks = w_grouped[:].rearrange("p (i h l c) -> p i h l c", i=UNITS, h=2, l=LOWS)

        def run(values):
            step = values[1] - values[0]
            assert all(b - a == step for a, b in zip(values, values[1:]))
            stop = values[-1] + (1 if step > 0 else -1)
            return slice(values[0], stop if stop >= 0 else None, step)

        def expand(i, scale_and_copy):
            upper, lower = i // LOWS, i % LOWS
            for sign in (1.0, -1.0):
                lows = [[l for l in range(LOWS) if table[(i, h * LOWS + l)][1] == sign] for h in range(2)]
                if lows[0] == lows[1]:
                    scale_and_copy(
                        w_blocks[:, i, :, run(lows[0]), :],
                        w_blocks[:, 0, run([upper, 1 - upper]), run([l ^ lower for l in lows[0]]), :],
                        sign,
                    )
                else:
                    for h in range(2):
                        if lows[h]:
                            scale_and_copy(
                                w_blocks[:, i, h, run(lows[h]), :],
                                w_blocks[:, 0, h ^ upper, run([l ^ lower for l in lows[h]]), :],
                                sign,
                            )

        def on_vector(dst, src, sign):
            nc.vector.tensor_scalar_mul(out=dst, in0=src, scalar1=sign)

        def on_scalar(dst, src, sign):
            nc.scalar.mul(dst, src, sign)

        expand(1, on_scalar)
        expand(4, on_scalar)
        n_cols = SIDES * F_OUT
        w_codes = const.tile([P, UNITS * n_cols], U32, name="w_codes", align_bytes=64)
        w_scales = const.tile([P, UNITS * n_cols], U8, name="w_scales", align_bytes=64)
        half = UNITS * n_cols // 2

        def quantise_weights(h):
            nc.vector.quantize_mx(
                out=w_codes[:, h * half : (h + 1) * half].bitcast(FP8X4),
                scales=w_scales[:, h * half : (h + 1) * half],
                in_=w_grouped[:, h * half * PACK : (h + 1) * half * PACK],
            )

        sorted_tiles = {}
        turned_tiles = {}
        grouped_tiles = {}
        code_tiles = {}
        acc_tiles = {}
        gate_tiles = {}
        out_tiles = {}

        def sort_words(r):
            sorted_words = sorted_pool.tile([P, UNITS, 2, QUARTER], F32, name="sorted_words")
            nc.vector.tensor_copy(
                out=sorted_words[:],
                in_=x_tiles[r][:].bitcast(F32).rearrange("p (c q w) -> p c q w", c=UNITS, q=QUARTERS)[
                    :, :, 0 : QUARTERS : QUARTERS - 1, :
                ],
            )
            sorted_tiles[r] = sorted_words

        def turn(r):
            outer = sorted_tiles[r]
            inner = x_tiles[r][:].bitcast(F32)
            banks = []
            for b in range(BANKS):
                xt = psum_t.tile([P, BANK_COMPS, 2, P], F32, name="xt")
                for c in range(BANK_COMPS):
                    comp = b * BANK_COMPS + c
                    nc.tensor.transpose(xt[:, c, 0, :], outer[:, comp].rearrange("p h w -> p (h w)"), ident[:])
                    nc.tensor.transpose(
                        xt[:, c, 1, :], inner[:, comp * 2 * P + QUARTER : comp * 2 * P + 3 * QUARTER], ident[:]
                    )
                banks.append(xt)
            turned_tiles[r] = banks
            grouped = grouped_pool.tile([P, features], BF16, name="grouped", align_bytes=64)
            grouped_tiles[r] = grouped

        def regroup(r, bank, copy):
            words = grouped_tiles[r][:].bitcast(F32).rearrange("p (c r u) -> p c r u", c=UNITS, u=2)
            copy(
                out=words[:, bank * BANK_COMPS : (bank + 1) * BANK_COMPS],
                in_=turned_tiles[r][bank][:].rearrange("p c u r -> p c r u"),
            )

        def transpose_and_regroup(r, vector_banks):
            turn(r)
            for b in range(BANKS):
                regroup(r, b, nc.vector.tensor_copy if b in vector_banks else nc.scalar.copy)

        def quantise(r):
            codes = codes_pool.tile([P, UNITS * P], U32, name="codes", align_bytes=64)
            scales = codes_pool.tile([P, UNITS * P], U8, name="scales", align_bytes=64)
            nc.vector.quantize_mx(
                out=codes[:].bitcast(FP8X4), scales=scales[:], in_=grouped_tiles[r][:]
            )
            code_tiles[r] = (codes, scales)

        def multiply(r, bank=None):
            if bank is None:
                if r % PAIR == 0 or r in firsts:
                    bank = psum_acc.tile([P, PAIR, n_cols], F32, name="acc")
                else:
                    bank = acc_tiles[r - 1]
            acc_tiles[r] = bank
            codes, scales = code_tiles[r]
            for i in range(UNITS):
                nc.tensor.matmul_mx(
                    out=bank[:, r % PAIR, :],
                    lhsT=codes[:, i * P : (i + 1) * P].bitcast(FP8X4),
                    lhsT_scale=scales[:, i * P : (i + 1) * P],
                    rhs=w_codes[:, i * n_cols : (i + 1) * n_cols].bitcast(FP8X4),
                    rhs_scale=w_scales[:, i * n_cols : (i + 1) * n_cols],
                    start=(i == 0),
                    stop=(i == UNITS - 1),
                )

        def by_side(r):
            return acc_tiles[r][:].rearrange("p t (k s o) -> p t k s o", k=UNITS, s=SIDES)

        def silu(tiles):
            t, n = tiles[0] % PAIR, len(tiles)
            gate = result_pool.tile([P, PAIR, F_OUT], F32, name="gate")
            nc.scalar.activation(
                out=gate[:, 0:n, :].rearrange("p t (k o) -> p t k o", k=UNITS),
                in_=by_side(tiles[0])[:, t : t + n, :, 0, :],
                func=SILU,
            )
            gate_tiles[tiles[0]] = gate

        def gate_product(tiles):
            h, n = tiles[0] % PAIR, len(tiles)
            g, t = tiles[0] // GROUP, tiles[0] % GROUP
            if t == 0:
                out_tiles[g] = result_pool.tile([P, GROUP, F_OUT], F32, name="out_sb")
            nc.vector.tensor_tensor(
                out=out_tiles[g][:, t : t + n, :].rearrange("p t (k o) -> p t k o", k=UNITS),
                in0=gate_tiles[tiles[0]][:, 0:n, :].rearrange("p t (k o) -> p t k o", k=UNITS),
                in1=by_side(tiles[0])[:, h : h + n, :, 1, :],
                op=MULT,
            )

        def store(g, first, count):
            nc.sync.dma_start(
                out=out_view[g][:, first * F_OUT : (first + count) * F_OUT],
                in_=out_tiles[g][:, first : first + count, :].rearrange("p t f -> p (t f)"),
            )

        def sort_to(last):
            for r in range(len(sorted_tiles), min(last, n_tiles - 1) + 1):
                sort_words(r)

        def quantise_to(last):
            for r in range(len(code_tiles), last + 1):
                quantise(r)

        def parts_to(end):
            parts = []
            r = progress["gated"]
            while r < end:
                n = PAIR if r % PAIR == 0 and r + 1 < end and r + 1 not in firsts else 1
                parts.append(list(range(r, r + n)))
                r += n
            progress["gated"] = end
            return parts

        def gate_to(end):
            parts = parts_to(end)
            for tiles in parts:
                silu(tiles)
            for tiles in parts:
                gate_product(tiles)

        def start_run(a):
            while (progress["stored"] + 1) * GROUP <= progress["gated"]:
                store(progress["stored"], 0, GROUP)
                progress["stored"] += 1
            if a > 0:
                for r in range(len(x_tiles), min(a + X_BUFS, n_tiles)):
                    x_tiles[r] = load(r)

        def multiply_to(end):
            for r in range(progress["multiplied"], end):
                multiply(r)
            progress["multiplied"] = end

        def pair_run(a):
            multiplied = progress["multiplied"]
            start_run(a)
            for r in (a, a + 1):
                if r == 1:
                    expand(6, on_vector)
                    expand(7, on_vector)
                sort_to(r + 1)
                if a == 0:
                    quantise_weights(r)
                if r >= 2:
                    quantise_to(r - 1)
                if r == n_tiles - PAIR:
                    gate_to(multiplied)
                transpose_and_regroup(r, (BANKS - 1,) if r == a and a >= 4 else ())
                if r == a:
                    gate_to(multiplied)

        def triple_run(a):
            on_act, on_dve = nc.scalar.copy, nc.vector.tensor_copy
            start_run(a)
            parts = parts_to(progress["multiplied"])
            sort_to(a + 1)
            for tiles in parts:
                silu(tiles)
            for tiles in parts:
                gate_product(tiles)
            turn(a)
            regroup(a, 0, on_act)
            regroup(a, 1, on_dve)
            regroup(a, 2, on_act)
            regroup(a, 3, on_dve)
            sort_to(a + 2)
            turn(a + 1)
            for b in range(BANKS):
                regroup(a + 1, b, on_act)
            quantise_to(a - 1)
            turn(a + 2)
            for b in range(BANKS):
                regroup(a + 2, b, on_act)
            quantise_to(a)
            sort_to(a + 3)
            quantise_to(a + 1)
            sort_to(a + (5))

        firsts = list(range(0, 12, 2)) + list(range(12, 30, 3)) + [30]
        progress = {"multiplied": 0, "gated": 0, "stored": 0}
        expand(2, on_vector)
        expand(3, on_vector)
        sort_words(0)
        expand(5, on_vector)
        a = 0
        for n in [2] * 6 + [3] * 6 + [2]:
            (pair_run if n == 2 else triple_run)(a)
            if a > 0:
                multiply_to(a)
            if a == 8:
                sort_to(11)
            if a == 10:
                sort_to(14)
            a += n
        last = n_tiles - PAIR
        quantise_to(n_tiles - 1)
        gate_to(last)
        for r in range(last, n_tiles):
            multiply(r, psum_t.tile([P, PAIR, n_cols], F32, name="xt"))
        start_run(0)
        for r in range(last, n_tiles):
            silu([r])
            gate_product([r])
            if r == n_tiles - 2:
                store(groups - 1, 0, GROUP - 1)
        store(groups - 1, GROUP - 1, 1)
